import numpy as np
import ml_dtypes


def mxq(x, axis, fmt="e4m3"):
    dtype, down = {"e4m3": (ml_dtypes.float8_e4m3fn, 7), "e5m2": (ml_dtypes.float8_e5m2, 14)}[fmt]
    v = np.moveaxis(np.asarray(x, np.float32).astype(ml_dtypes.bfloat16).astype(np.float64), axis, -1)
    blocks = v.reshape(v.shape[:-1] + (-1, 32))
    amax = np.abs(blocks).max(-1, keepdims=True)
    byte = np.maximum(np.where(amax > 0, np.frexp(amax)[1] - 1 + 127, 0) - down, 1)
    scale = np.exp2(byte - 127.0)
    codes = (blocks / scale).astype(np.float32).astype(dtype).astype(np.float64)
    return np.moveaxis((codes * scale).reshape(v.shape), -1, axis)


WIDE = False


def mx_kscale(k):
    if not WIDE:
        return np.ones(k)
    levels = np.array([10, -10, 5, -5, 0])
    a = np.random.permutation(np.resize(levels, k // 512 * 4)).reshape(k // 512, 4)
    idx = np.arange(k)
    return np.exp2(a[idx // 512, idx % 128 // 32])


BF16 = ml_dtypes.bfloat16


def bf(x):
    return np.asarray(x, np.float32).astype(BF16)


def f64(x):
    return np.asarray(x).astype(np.float64)


B, S, H, NH, HD = 1, 512, 2048, 16, 128
E = NH * HD


def heads(t):
    return t.reshape(B, S, NH, HD).transpose(0, 2, 1, 3)


def setup_inputs():
    s = mx_kscale(H)
    c = S ** -0.25
    return {"hidden_states": bf(np.random.standard_normal((B, S, H)) * s),
            "Wk": bf(np.random.standard_normal((H, E)) * c / np.sqrt(H) / s[:, None]),
            "bk": bf(np.random.standard_normal(E) / np.sqrt(S)),
            "Wv": bf(np.random.standard_normal((H, E)) * c / np.sqrt(H) / s[:, None]),
            "bv": bf(np.random.standard_normal(E) / np.sqrt(S))}


def reference(hidden_states, Wk, bk, Wv, bv):
    xq = mxq(f64(hidden_states), 2, "e4m3")
    k = heads((xq @ mxq(f64(Wk), 0, "e4m3")) + f64(bk))
    v = heads((xq @ mxq(f64(Wv), 0, "e4m3")) + f64(bv))
    return mxq(k, 2, "e4m3").transpose(0, 1, 3, 2) @ mxq(v, 2, "e4m3")

@@ -1,0 +1,266 @@
+from contextlib import ExitStack
+
+import concourse.mybir as mybir
+from concourse.masks import make_identity
+
+BF16 = mybir.dt.bfloat16
+F32 = mybir.dt.float32
+U32 = mybir.dt.uint32
+U8 = mybir.dt.uint8
+FP8X4 = mybir.dt.float8_e4m3fn_x4
+
+P = 128
+PACK = 4
+K_PASS = P * PACK
+
+S = 512
+H = 2048
+HEADS = 16
+HD = 128
+E = HEADS * HD
+
+PASSES = H // K_PASS
+ROW_TILES = S // P
+BANK = 512
+
+LOAD_HEADS = 8
+LOAD_COLS = LOAD_HEADS * HD
+RAW_BUFS = 8
+GROUP = 4
+
+UNITS = ((0, 0, 8), (1, 0, 8), (0, 8, 8), (1, 8, 4), (1, 12, 4))
+
+SCALAR_SIXTEENTHS_EARLY = 8
+SCALAR_SIXTEENTHS = 12
+
+FLOPS = 2 * S * H * 2 * E + 2 * HEADS * HD * HD * S
+
+
+def tile_linearattention_pa_kernel(tc, hidden_states, Wk, bk, Wv, bv, out):
+    nc = tc.nc
+    weights = (Wk, Wv)
+    biases = (bk, bv)
+
+    with ExitStack() as ctx:
+        ctx.enter_context(tc.manual_schedule())
+        keep = ctx.enter_context(tc.tile_pool(name="keep", bufs=1))
+        raw_pool = ctx.enter_context(tc.tile_pool(name="raw", bufs=RAW_BUFS))
+        grouped_pool = ctx.enter_context(tc.tile_pool(name="grouped", bufs=3))
+        wq_pool = ctx.enter_context(tc.tile_pool(name="wq", bufs=2))
+        heads_pool = ctx.enter_context(tc.tile_pool(name="heads", bufs=3))
+        result_pool = ctx.enter_context(tc.tile_pool(name="result", bufs=2))
+        banks = ctx.enter_context(tc.psum_pool(name="banks", bufs=6))
+        state_banks = ctx.enter_context(tc.psum_pool(name="state_banks", bufs=2))
+
+        identity = keep.tile([P, P], F32, name="identity")
+        x_raw = keep.tile([P, ROW_TILES, H], BF16, name="x_raw")
+        x_grouped = keep.tile([P, PASSES * S * PACK], BF16, name="x_grouped", align_bytes=64)
+        x_codes = keep.tile([P, PASSES, S], U32, name="x_codes", align_bytes=64)
+        x_scales = keep.tile([P, PASSES, S], U8, name="x_scales", align_bytes=64)
+        bias_rows = keep.tile([P, 2, E], BF16, name="bias_rows")
+        kv_codes = keep.tile([P, 2, E], U32, name="kv_codes", align_bytes=64)
+        kv_scales = keep.tile([P, 2, E], U8, name="kv_scales", align_bytes=64)
+
+        make_identity(nc, identity[:])
+
+        x_rows = hidden_states[0].rearrange("(p t) h -> p t h", t=ROW_TILES)
+        for t in range(ROW_TILES):
+            nc.sync.dma_start(out=x_raw[:, t, :], in_=x_rows[:, t, :])
+
+        pieces = [
+            (w, first_head // LOAD_HEADS, c)
+            for (w, first_head, n_heads) in UNITS
+            if first_head % LOAD_HEADS == 0
+            for c in range(PASSES)
+        ]
+        raw_tiles = {}
+
+        def load_piece(index):
+            w, half, c = pieces[index]
+            raw = raw_pool.tile([P, PACK, LOAD_COLS], BF16, name="raw")
+            rows = weights[w].rearrange("(c p j) n -> c p j n", p=P, j=PACK)
+            nc.sync.dma_start(
+                out=raw[:], in_=rows[c][:, :, half * LOAD_COLS : (half + 1) * LOAD_COLS]
+            )
+            raw_tiles[pieces[index]] = raw
+
+        def load_bias(w):
+            nc.sync.dma_start(out=bias_rows[:, w, :], in_=biases[w].partition_broadcast(P))
+
+        for index in range(RAW_BUFS):
+            load_piece(index)
+            if index % PASSES == PASSES - 1:
+                load_bias(index // PASSES)
+
+        x_words = x_raw[:].bitcast(F32).rearrange(
+            "p t (c w u) -> p t c u w", c=PASSES, u=2
+        )
+        xg_words = x_grouped[:].bitcast(F32).rearrange(
+            "p (c t m u) -> p c t m u", c=PASSES, t=ROW_TILES, u=2
+        )
+        for t in range(ROW_TILES):
+            for half in range(2):
+                bank = banks.tile([P, BANK], F32, name="bank")
+                planes = bank[:].rearrange("p (c u m) -> p c u m", c=2, u=2)
+                for c in range(2):
+                    for u in range(2):
+                        nc.tensor.transpose(
+                            planes[:, c, u, :], x_words[:, t, 2 * half + c, u, :], identity[:]
+                        )
+                copy = nc.scalar.copy if half == 0 else nc.vector.tensor_copy
+                copy(
+                    out=xg_words[:, 2 * half : 2 * half + 2, t, :, :],
+                    in_=planes.rearrange("p c u m -> p c m u"),
+                )
+        for c in range(PASSES):
+            nc.vector.quantize_mx(
+                out=x_codes[:, c, :].bitcast(FP8X4),
+                scales=x_scales[:, c, :],
+                in_=x_grouped[:, c * S * PACK : (c + 1) * S * PACK],
+            )
+
+        slots = [(u, c) for u in range(len(UNITS)) for c in range(PASSES)]
+        grouped_tiles = {}
+        wq_tiles = {}
+        bank_tiles = {}
+        head_tiles = {}
+        state_tiles = {}
+
+        def regroup(u, c, scalar_sixteenths):
+            w, first_head, n_heads = UNITS[u]
+            cols = n_heads * HD
+            start = (first_head % LOAD_HEADS) * HD
+            raw = raw_tiles[(w, first_head // LOAD_HEADS, c)]
+            grouped = grouped_pool.tile([P, cols, PACK], BF16, name="grouped", align_bytes=64)
+            split = cols * scalar_sixteenths // 16
+            for copy, lo, hi in ((nc.scalar.copy, 0, split), (nc.vector.tensor_copy, split, cols)):
+                copy(
+                    out=grouped[:, lo:hi, :].rearrange("p (g i) j -> p g j i", i=4),
+                    in_=raw[:, :, start + lo : start + hi].rearrange("p j (g i) -> p g j i", i=4),
+                )
+            grouped_tiles[(u, c)] = grouped
+
+        def quantise_weights(u, c):
+            cols = UNITS[u][2] * HD
+            if c == 0:
+                w_codes = wq_pool.tile([P, PASSES, cols], U32, name="w_codes", align_bytes=64)
+                w_scales = wq_pool.tile([P, PASSES, cols], U8, name="w_scales", align_bytes=64)
+                wq_tiles[u] = (w_codes, w_scales)
+            w_codes, w_scales = wq_tiles[u]
+            nc.vector.quantize_mx(
+                out=w_codes[:, c, :].bitcast(FP8X4),
+                scales=w_scales[:, c, :],
+                in_=grouped_tiles[(u, c)][:].rearrange("p n j -> p (n j)"),
+            )
+
+        def project(u, local_head):
+            w_codes, w_scales = wq_tiles[u]
+            cols = slice(local_head * HD, (local_head + 1) * HD)
+            bank = banks.tile([P, BANK], F32, name="bank")
+            for t in range(ROW_TILES):
+                rows = slice(t * P, (t + 1) * P)
+                for c in range(PASSES):
+                    nc.tensor.matmul_mx(
+                        out=bank[:, t * HD : (t + 1) * HD],
+                        lhsT=x_codes[:, c, rows].bitcast(FP8X4),
+                        lhsT_scale=x_scales[:, c, rows],
+                        rhs=w_codes[:, c, cols].bitcast(FP8X4),
+                        rhs_scale=w_scales[:, c, cols],
+                        start=(c == 0),
+                        stop=(c == PASSES - 1),
+                    )
+            bank_tiles[(u, local_head)] = bank
+
+        def add_bias(u, local_head):
+            w, first_head, n_heads = UNITS[u]
+            head = first_head + local_head
+            if head % GROUP == 0:
+                head_tiles[(w, head // GROUP)] = heads_pool.tile(
+                    [P, GROUP * HD, PACK], BF16, name="heads_grouped", align_bytes=64
+                )
+            heads_grouped = head_tiles[(w, head // GROUP)]
+            place = (head % GROUP) * HD
+            nc.vector.tensor_tensor(
+                out=heads_grouped[:, place : place + HD, :],
+                in0=bank_tiles[(u, local_head)][:].rearrange("p (t n) -> p n t", t=ROW_TILES),
+                in1=bias_rows[:, w, head * HD : (head + 1) * HD]
+                .unsqueeze(2)
+                .to_broadcast([P, HD, PACK]),
+                op=mybir.AluOpType.add,
+            )
+
+        def quantise_heads(w, group):
+            cols = slice(group * GROUP * HD, (group + 1) * GROUP * HD)
+            nc.vector.quantize_mx(
+                out=kv_codes[:, w, cols].bitcast(FP8X4),
+                scales=kv_scales[:, w, cols],
+                in_=head_tiles[(w, group)][:].rearrange("p n t -> p (n t)"),
+            )
+
+        def state(group):
+            bank = state_banks.tile([P, GROUP, HD], F32, name="state_bank")
+            for g in range(GROUP):
+                cols = slice((group * GROUP + g) * HD, (group * GROUP + g + 1) * HD)
+                nc.tensor.matmul_mx(
+                    out=bank[:, g, :],
+                    lhsT=kv_codes[:, 0, cols].bitcast(FP8X4),
+                    lhsT_scale=kv_scales[:, 0, cols],
+                    rhs=kv_codes[:, 1, cols].bitcast(FP8X4),
+                    rhs_scale=kv_scales[:, 1, cols],
+                    start=True,
+                    stop=True,
+                )
+            state_tiles[group] = bank
+
+        def store_state(group):
+            result = result_pool.tile([P, GROUP, HD], F32, name="result")
+            nc.scalar.copy(out=result[:], in_=state_tiles[group][:])
+            nc.sync.dma_start(
+                out=out[0, group * GROUP : (group + 1) * GROUP].rearrange("h d e -> d h e"),
+                in_=result[:],
+            )
+
+        def step_heads(slot):
+            u, step = slots[slot]
+            per_step = UNITS[u][2] // PASSES
+            return u, range(step * per_step, (step + 1) * per_step)
+
+        def finished_groups(slot):
+            u, local_heads = step_heads(slot)
+            w, first_head, n_heads = UNITS[u]
+            return [
+                (w, (first_head + local_head) // GROUP)
+                for local_head in local_heads
+                if (first_head + local_head) % GROUP == GROUP - 1
+            ]
+
+        QUANTISE_LAG = 1
+        PROJECT_LAG = PASSES
+        BIAS_LAG = PROJECT_LAG + 1
+        STATE_LAG = BIAS_LAG + 1
+        STORE_LAG = STATE_LAG + 1
+        n_slots = len(slots)
+        for q in range(n_slots + STORE_LAG):
+            if 0 <= q - STATE_LAG < n_slots:
+                for w, group in finished_groups(q - STATE_LAG):
+                    quantise_heads(w, group)
+                    if w == 1:
+                        state(group)
+            if 0 <= q - QUANTISE_LAG < n_slots:
+                quantise_weights(*slots[q - QUANTISE_LAG])
+            if q < n_slots:
+                regroup(*slots[q], SCALAR_SIXTEENTHS_EARLY if q < BIAS_LAG else SCALAR_SIXTEENTHS)
+                if q + RAW_BUFS < len(pieces):
+                    load_piece(q + RAW_BUFS)
+            if 0 <= q - PROJECT_LAG < n_slots:
+                u, local_heads = step_heads(q - PROJECT_LAG)
+                for local_head in local_heads:
+                    project(u, local_head)
+            if 0 <= q - BIAS_LAG < n_slots:
+                u, local_heads = step_heads(q - BIAS_LAG)
+                for local_head in local_heads:
+                    add_bias(u, local_head)
+            if 0 <= q - STORE_LAG < n_slots:
+                for w, group in finished_groups(q - STORE_LAG):
+                    if w == 1:
+                        store_state(group)

@@ -42,7 +42,6 @@ def tile_linearattention_pa_kernel(tc, hidden_states, Wk, bk, Wv, bv, out):
     biases = (bk, bv)
 
     with ExitStack() as ctx:
-        ctx.enter_context(tc.manual_schedule())
         keep = ctx.enter_context(tc.tile_pool(name="keep", bufs=1))
         raw_pool = ctx.enter_context(tc.tile_pool(name="raw", bufs=RAW_BUFS))
         grouped_pool = ctx.enter_context(tc.tile_pool(name="grouped", bufs=3))

@@ -23,15 +23,19 @@ PASSES = H // K_PASS
 ROW_TILES = S // P
 BANK = 512
 
-LOAD_HEADS = 8
-LOAD_COLS = LOAD_HEADS * HD
-RAW_BUFS = 8
-GROUP = 4
+BLOCKS = ((0, 0, 4), (1, 0, 4), (0, 4, 8), (1, 4, 8), (0, 12, 4), (1, 12, 4))
 
-UNITS = ((0, 0, 8), (1, 0, 8), (0, 8, 8), (1, 8, 4), (1, 12, 4))
+UNITS = (
+    (0, 0, 4), (1, 0, 4), (2, 4, 4), (2, 8, 4), (3, 4, 4), (3, 8, 4),
+    (4, 12, 4), (5, 12, 2), (5, 14, 1), (5, 15, 1),
+)
 
-SCALAR_SIXTEENTHS_EARLY = 8
-SCALAR_SIXTEENTHS = 12
+STORE_LAG = 2
+
+ROUND_COLS = 512
+
+SCALAR_COLS_EARLY = 256
+SCALAR_COLS = 384
 
 FLOPS = 2 * S * H * 2 * E + 2 * HEADS * HD * HD * S
 
@@ -43,13 +47,15 @@ def tile_linearattention_pa_kernel(tc, hidden_states, Wk, bk, Wv, bv, out):
 
     with ExitStack() as ctx:
         keep = ctx.enter_context(tc.tile_pool(name="keep", bufs=1))
-        raw_pool = ctx.enter_context(tc.tile_pool(name="raw", bufs=RAW_BUFS))
-        grouped_pool = ctx.enter_context(tc.tile_pool(name="grouped", bufs=3))
-        wq_pool = ctx.enter_context(tc.tile_pool(name="wq", bufs=2))
+        narrow_pool = ctx.enter_context(tc.tile_pool(name="narrow", bufs=2 * PASSES))
+        wide_pool = ctx.enter_context(tc.tile_pool(name="wide", bufs=2 * PASSES))
+        grouped_pool = ctx.enter_context(tc.tile_pool(name="grouped", bufs=4))
+        wq_pool = ctx.enter_context(tc.tile_pool(name="wq", bufs=3))
         heads_pool = ctx.enter_context(tc.tile_pool(name="heads", bufs=3))
-        result_pool = ctx.enter_context(tc.tile_pool(name="result", bufs=2))
+        result_pool = ctx.enter_context(tc.tile_pool(name="result", bufs=4))
         banks = ctx.enter_context(tc.psum_pool(name="banks", bufs=6))
         state_banks = ctx.enter_context(tc.psum_pool(name="state_banks", bufs=2))
+        ctx.enter_context(tc.manual_schedule())
 
         identity = keep.tile([P, P], F32, name="identity")
         x_raw = keep.tile([P, ROW_TILES, H], BF16, name="x_raw")
@@ -62,34 +68,43 @@ def tile_linearattention_pa_kernel(tc, hidden_states, Wk, bk, Wv, bv, out):
 
         make_identity(nc, identity[:])
 
-        x_rows = hidden_states[0].rearrange("(p t) h -> p t h", t=ROW_TILES)
-        for t in range(ROW_TILES):
-            nc.sync.dma_start(out=x_raw[:, t, :], in_=x_rows[:, t, :])
-
-        pieces = [
-            (w, first_head // LOAD_HEADS, c)
-            for (w, first_head, n_heads) in UNITS
-            if first_head % LOAD_HEADS == 0
-            for c in range(PASSES)
-        ]
         raw_tiles = {}
 
-        def load_piece(index):
-            w, half, c = pieces[index]
-            raw = raw_pool.tile([P, PACK, LOAD_COLS], BF16, name="raw")
+        def load_piece(block, c):
+            w, first_head, n_heads = BLOCKS[block]
+            cols = n_heads * HD
+            if n_heads == 4:
+                raw = narrow_pool.tile([P, PACK, cols], BF16, name="raw_narrow")
+            else:
+                raw = wide_pool.tile([P, PACK, cols], BF16, name="raw_wide")
             rows = weights[w].rearrange("(c p j) n -> c p j n", p=P, j=PACK)
             nc.sync.dma_start(
-                out=raw[:], in_=rows[c][:, :, half * LOAD_COLS : (half + 1) * LOAD_COLS]
+                out=raw[:], in_=rows[c][:, :, first_head * HD : first_head * HD + cols]
             )
-            raw_tiles[pieces[index]] = raw
+            raw_tiles[(block, c)] = raw
 
         def load_bias(w):
             nc.sync.dma_start(out=bias_rows[:, w, :], in_=biases[w].partition_broadcast(P))
 
-        for index in range(RAW_BUFS):
-            load_piece(index)
-            if index % PASSES == PASSES - 1:
-                load_bias(index // PASSES)
+        x_rows = hidden_states[0].rearrange("(p t) h -> p t h", t=ROW_TILES)
+
+        def load_x(t):
+            nc.sync.dma_start(out=x_raw[:, t, :], in_=x_rows[:, t, :])
+
+        load_piece(0, 0)
+        load_piece(0, 1)
+        for t in range(ROW_TILES):
+            load_x(t)
+        load_piece(0, 2)
+        load_piece(0, 3)
+        for c in range(PASSES):
+            load_piece(1, c)
+        load_bias(0)
+        for c in range(PASSES):
+            load_piece(2, c)
+        load_bias(1)
+        for c in range(PASSES):
+            load_piece(3, c)
 
         x_words = x_raw[:].bitcast(F32).rearrange(
             "p t (c w u) -> p t c u w", c=PASSES, u=2
@@ -97,7 +112,8 @@ def tile_linearattention_pa_kernel(tc, hidden_states, Wk, bk, Wv, bv, out):
         xg_words = x_grouped[:].bitcast(F32).rearrange(
             "p (c t m u) -> p c t m u", c=PASSES, t=ROW_TILES, u=2
         )
-        for t in range(ROW_TILES):
+
+        def transpose_x(t):
             for half in range(2):
                 bank = banks.tile([P, BANK], F32, name="bank")
                 planes = bank[:].rearrange("p (c u m) -> p c u m", c=2, u=2)
@@ -111,74 +127,94 @@ def tile_linearattention_pa_kernel(tc, hidden_states, Wk, bk, Wv, bv, out):
                     out=xg_words[:, 2 * half : 2 * half + 2, t, :, :],
                     in_=planes.rearrange("p c u m -> p c m u"),
                 )
-        for c in range(PASSES):
+
+        def quantise_x(c):
             nc.vector.quantize_mx(
                 out=x_codes[:, c, :].bitcast(FP8X4),
                 scales=x_scales[:, c, :],
                 in_=x_grouped[:, c * S * PACK : (c + 1) * S * PACK],
             )
 
-        slots = [(u, c) for u in range(len(UNITS)) for c in range(PASSES)]
+        rounds = []
+        last_round = {}
+        for u, (block, first_head, n_heads) in enumerate(UNITS):
+            per_round = ROUND_COLS // (n_heads * HD)
+            for c in range(0, PASSES, per_round):
+                last_round[u] = len(rounds)
+                rounds.append((u, range(c, c + per_round)))
         grouped_tiles = {}
         wq_tiles = {}
         bank_tiles = {}
         head_tiles = {}
         state_tiles = {}
 
-        def regroup(u, c, scalar_sixteenths):
-            w, first_head, n_heads = UNITS[u]
+        def regroup(r, scalar_cols):
+            u, passes = rounds[r]
+            block, first_head, n_heads = UNITS[u]
             cols = n_heads * HD
-            start = (first_head % LOAD_HEADS) * HD
-            raw = raw_tiles[(w, first_head // LOAD_HEADS, c)]
-            grouped = grouped_pool.tile([P, cols, PACK], BF16, name="grouped", align_bytes=64)
-            split = cols * scalar_sixteenths // 16
-            for copy, lo, hi in ((nc.scalar.copy, 0, split), (nc.vector.tensor_copy, split, cols)):
-                copy(
-                    out=grouped[:, lo:hi, :].rearrange("p (g i) j -> p g j i", i=4),
-                    in_=raw[:, :, start + lo : start + hi].rearrange("p j (g i) -> p g j i", i=4),
-                )
-            grouped_tiles[(u, c)] = grouped
+            start = (first_head - BLOCKS[block][1]) * HD
+            grouped = grouped_pool.tile([P, ROUND_COLS, PACK], BF16, name="grouped", align_bytes=64)
+            for i, c in enumerate(passes):
+                raw = raw_tiles[(block, c)]
+                split = min(max(scalar_cols - i * cols, 0), cols)
+                for copy, lo, hi in (
+                    (nc.scalar.copy, 0, split), (nc.vector.tensor_copy, split, cols),
+                ):
+                    if lo < hi:
+                        copy(
+                            out=grouped[:, i * cols + lo : i * cols + hi, :].rearrange(
+                                "p (g i) j -> p g j i", i=4
+                            ),
+                            in_=raw[:, :, start + lo : start + hi].rearrange(
+                                "p j (g i) -> p g j i", i=4
+                            ),
+                        )
+            grouped_tiles[r] = grouped
 
-        def quantise_weights(u, c):
+        def quantise_weights(r):
+            u, passes = rounds[r]
             cols = UNITS[u][2] * HD
-            if c == 0:
-                w_codes = wq_pool.tile([P, PASSES, cols], U32, name="w_codes", align_bytes=64)
-                w_scales = wq_pool.tile([P, PASSES, cols], U8, name="w_scales", align_bytes=64)
+            if passes[0] == 0:
+                w_codes = wq_pool.tile([P, PASSES * cols], U32, name="w_codes", align_bytes=64)
+                w_scales = wq_pool.tile([P, PASSES * cols], U8, name="w_scales", align_bytes=64)
                 wq_tiles[u] = (w_codes, w_scales)
             w_codes, w_scales = wq_tiles[u]
+            words = slice(passes[0] * cols, passes[0] * cols + ROUND_COLS)
             nc.vector.quantize_mx(
-                out=w_codes[:, c, :].bitcast(FP8X4),
-                scales=w_scales[:, c, :],
-                in_=grouped_tiles[(u, c)][:].rearrange("p n j -> p (n j)"),
+                out=w_codes[:, words].bitcast(FP8X4),
+                scales=w_scales[:, words],
+                in_=grouped_tiles[r][:].rearrange("p n j -> p (n j)"),
             )
 
         def project(u, local_head):
             w_codes, w_scales = wq_tiles[u]
-            cols = slice(local_head * HD, (local_head + 1) * HD)
+            cols = UNITS[u][2] * HD
             bank = banks.tile([P, BANK], F32, name="bank")
             for t in range(ROW_TILES):
                 rows = slice(t * P, (t + 1) * P)
                 for c in range(PASSES):
+                    words = slice(c * cols + local_head * HD, c * cols + (local_head + 1) * HD)
                     nc.tensor.matmul_mx(
                         out=bank[:, t * HD : (t + 1) * HD],
                         lhsT=x_codes[:, c, rows].bitcast(FP8X4),
                         lhsT_scale=x_scales[:, c, rows],
-                        rhs=w_codes[:, c, cols].bitcast(FP8X4),
-                        rhs_scale=w_scales[:, c, cols],
+                        rhs=w_codes[:, words].bitcast(FP8X4),
+                        rhs_scale=w_scales[:, words],
                         start=(c == 0),
                         stop=(c == PASSES - 1),
                     )
             bank_tiles[(u, local_head)] = bank
 
         def add_bias(u, local_head):
-            w, first_head, n_heads = UNITS[u]
+            block, first_head, n_heads = UNITS[u]
+            w = BLOCKS[block][0]
             head = first_head + local_head
-            if head % GROUP == 0:
-                head_tiles[(w, head // GROUP)] = heads_pool.tile(
-                    [P, GROUP * HD, PACK], BF16, name="heads_grouped", align_bytes=64
+            if local_head == 0:
+                head_tiles[u] = heads_pool.tile(
+                    [P, n_heads * HD, PACK], BF16, name="heads_grouped", align_bytes=64
                 )
-            heads_grouped = head_tiles[(w, head // GROUP)]
-            place = (head % GROUP) * HD
+            heads_grouped = head_tiles[u]
+            place = local_head * HD
             nc.vector.tensor_tensor(
                 out=heads_grouped[:, place : place + HD, :],
                 in0=bank_tiles[(u, local_head)][:].rearrange("p (t n) -> p n t", t=ROW_TILES),
@@ -188,18 +224,21 @@ def tile_linearattention_pa_kernel(tc, hidden_states, Wk, bk, Wv, bv, out):
                 op=mybir.AluOpType.add,
             )
 
-        def quantise_heads(w, group):
-            cols = slice(group * GROUP * HD, (group + 1) * GROUP * HD)
+        def quantise_heads(u):
+            block, first_head, n_heads = UNITS[u]
+            w = BLOCKS[block][0]
+            cols = slice(first_head * HD, (first_head + n_heads) * HD)
             nc.vector.quantize_mx(
                 out=kv_codes[:, w, cols].bitcast(FP8X4),
                 scales=kv_scales[:, w, cols],
-                in_=head_tiles[(w, group)][:].rearrange("p n t -> p (n t)"),
+                in_=head_tiles[u][:].rearrange("p n t -> p (n t)"),
             )
 
-        def state(group):
-            bank = state_banks.tile([P, GROUP, HD], F32, name="state_bank")
-            for g in range(GROUP):
-                cols = slice((group * GROUP + g) * HD, (group * GROUP + g + 1) * HD)
+        def state(u):
+            block, first_head, n_heads = UNITS[u]
+            bank = state_banks.tile([P, n_heads, HD], F32, name="state_bank")
+            for g in range(n_heads):
+                cols = slice((first_head + g) * HD, (first_head + g + 1) * HD)
                 nc.tensor.matmul_mx(
                     out=bank[:, g, :],
                     lhsT=kv_codes[:, 0, cols].bitcast(FP8X4),
@@ -209,57 +248,52 @@ def tile_linearattention_pa_kernel(tc, hidden_states, Wk, bk, Wv, bv, out):
                     start=True,
                     stop=True,
                 )
-            state_tiles[group] = bank
+            state_tiles[u] = bank
 
-        def store_state(group):
-            result = result_pool.tile([P, GROUP, HD], F32, name="result")
-            nc.scalar.copy(out=result[:], in_=state_tiles[group][:])
+        def store_state(u):
+            block, first_head, n_heads = UNITS[u]
+            result = result_pool.tile([P, n_heads, HD], F32, name="result")
+            nc.scalar.copy(out=result[:], in_=state_tiles[u][:])
             nc.sync.dma_start(
-                out=out[0, group * GROUP : (group + 1) * GROUP].rearrange("h d e -> d h e"),
+                out=out[0, first_head : first_head + n_heads].rearrange("h d e -> d h e"),
                 in_=result[:],
             )
 
-        def step_heads(slot):
-            u, step = slots[slot]
-            per_step = UNITS[u][2] // PASSES
-            return u, range(step * per_step, (step + 1) * per_step)
-
-        def finished_groups(slot):
-            u, local_heads = step_heads(slot)
-            w, first_head, n_heads = UNITS[u]
-            return [
-                (w, (first_head + local_head) // GROUP)
-                for local_head in local_heads
-                if (first_head + local_head) % GROUP == GROUP - 1
-            ]
-
-        QUANTISE_LAG = 1
-        PROJECT_LAG = PASSES
-        BIAS_LAG = PROJECT_LAG + 1
-        STATE_LAG = BIAS_LAG + 1
-        STORE_LAG = STATE_LAG + 1
-        n_slots = len(slots)
-        for q in range(n_slots + STORE_LAG):
-            if 0 <= q - STATE_LAG < n_slots:
-                for w, group in finished_groups(q - STATE_LAG):
-                    quantise_heads(w, group)
-                    if w == 1:
-                        state(group)
-            if 0 <= q - QUANTISE_LAG < n_slots:
-                quantise_weights(*slots[q - QUANTISE_LAG])
-            if q < n_slots:
-                regroup(*slots[q], SCALAR_SIXTEENTHS_EARLY if q < BIAS_LAG else SCALAR_SIXTEENTHS)
-                if q + RAW_BUFS < len(pieces):
-                    load_piece(q + RAW_BUFS)
-            if 0 <= q - PROJECT_LAG < n_slots:
-                u, local_heads = step_heads(q - PROJECT_LAG)
-                for local_head in local_heads:
-                    project(u, local_head)
-            if 0 <= q - BIAS_LAG < n_slots:
-                u, local_heads = step_heads(q - BIAS_LAG)
-                for local_head in local_heads:
-                    add_bias(u, local_head)
-            if 0 <= q - STORE_LAG < n_slots:
-                for w, group in finished_groups(q - STORE_LAG):
-                    if w == 1:
-                        store_state(group)
+        to_project = {}
+        to_bias = {}
+        to_finish = {}
+        to_store = {}
+        for u, (block, first_head, n_heads) in enumerate(UNITS):
+            for local_head in range(n_heads):
+                q = last_round[u] + 1 + local_head
+                to_project.setdefault(q, []).append((u, local_head))
+                to_bias.setdefault(q + 1, []).append((u, local_head))
+            to_finish.setdefault(q + 2, []).append(u)
+            if BLOCKS[block][0] == 1:
+                to_store.setdefault(q + 2 + STORE_LAG, []).append(u)
+        n_rounds = max(to_store) + 1
+        late_blocks = [(block, c) for block in (4, 5) for c in range(PASSES)]
+        for q in range(n_rounds):
+            if 0 < q <= len(rounds):
+                quantise_weights(q - 1)
+            for u in to_finish.get(q, []):
+                quantise_heads(u)
+            if q < len(rounds):
+                regroup(q, SCALAR_COLS_EARLY if q < 5 else SCALAR_COLS)
+            if q == 1:
+                for t in range(ROW_TILES):
+                    transpose_x(t)
+            if q == 2:
+                for c in range(PASSES):
+                    quantise_x(c)
+            if q >= 8 and late_blocks:
+                load_piece(*late_blocks.pop(0))
+            for u, local_head in to_project.get(q, []):
+                project(u, local_head)
+            for u in to_finish.get(q, []):
+                if BLOCKS[UNITS[u][0]][0] == 1:
+                    state(u)
+            for u, local_head in to_bias.get(q, []):
+                add_bias(u, local_head)
+            for u in to_store.get(q, []):
+                store_state(u)

@@ -23,19 +23,20 @@ PASSES = H // K_PASS
 ROW_TILES = S // P
 BANK = 512
 
-BLOCKS = ((0, 0, 4), (1, 0, 4), (0, 4, 8), (1, 4, 8), (0, 12, 4), (1, 12, 4))
+BLOCKS = ((0, 0, 4), (1, 0, 4), (0, 4, 4), (1, 4, 4), (0, 8, 4), (1, 8, 4), (0, 12, 4), (1, 12, 4))
 
 UNITS = (
-    (0, 0, 4), (1, 0, 4), (2, 4, 4), (2, 8, 4), (3, 4, 4), (3, 8, 4),
-    (4, 12, 4), (5, 12, 2), (5, 14, 1), (5, 15, 1),
+    (0, 0, 4), (1, 0, 4), (2, 4, 4), (3, 4, 4), (4, 8, 4), (5, 8, 4), (6, 12, 4),
+    (7, 12, 2), (7, 14, 1), (7, 15, 1),
 )
 
-STORE_LAG = 2
-
-ROUND_COLS = 512
-
-SCALAR_COLS_EARLY = 256
-SCALAR_COLS = 384
+ROUND_COLS = 1024
+FIRST_ROUNDS = 3
+SHARES_EARLY = (512, 512, 0, 0)
+SHARES = (704, 320, 0, 0)
+SHARES_LAST = (640, 384, 0, 0)
+AHEAD = 3
+STORE_LAG = 1
 
 FLOPS = 2 * S * H * 2 * E + 2 * HEADS * HD * HD * S
 
@@ -47,129 +48,191 @@ def tile_linearattention_pa_kernel(tc, hidden_states, Wk, bk, Wv, bv, out):
 
     with ExitStack() as ctx:
         keep = ctx.enter_context(tc.tile_pool(name="keep", bufs=1))
-        narrow_pool = ctx.enter_context(tc.tile_pool(name="narrow", bufs=2 * PASSES))
-        wide_pool = ctx.enter_context(tc.tile_pool(name="wide", bufs=2 * PASSES))
-        grouped_pool = ctx.enter_context(tc.tile_pool(name="grouped", bufs=4))
-        wq_pool = ctx.enter_context(tc.tile_pool(name="wq", bufs=3))
-        heads_pool = ctx.enter_context(tc.tile_pool(name="heads", bufs=3))
+        raw_pool = ctx.enter_context(tc.tile_pool(name="raw", bufs=24))
+        grouped_pool = ctx.enter_context(tc.tile_pool(name="grouped", bufs=AHEAD))
+        wq_pool = ctx.enter_context(tc.tile_pool(name="wq", bufs=2))
+        heads_pool = ctx.enter_context(tc.tile_pool(name="heads", bufs=4))
         result_pool = ctx.enter_context(tc.tile_pool(name="result", bufs=4))
-        banks = ctx.enter_context(tc.psum_pool(name="banks", bufs=6))
-        state_banks = ctx.enter_context(tc.psum_pool(name="state_banks", bufs=2))
+        banks = ctx.enter_context(tc.psum_pool(name="banks", bufs=5))
+        move_banks = ctx.enter_context(tc.psum_pool(name="move_banks", bufs=2))
+        state_banks = ctx.enter_context(tc.psum_pool(name="state_banks", bufs=1))
         ctx.enter_context(tc.manual_schedule())
 
         identity = keep.tile([P, P], F32, name="identity")
-        x_raw = keep.tile([P, ROW_TILES, H], BF16, name="x_raw")
-        x_grouped = keep.tile([P, PASSES * S * PACK], BF16, name="x_grouped", align_bytes=64)
         x_codes = keep.tile([P, PASSES, S], U32, name="x_codes", align_bytes=64)
         x_scales = keep.tile([P, PASSES, S], U8, name="x_scales", align_bytes=64)
         bias_rows = keep.tile([P, 2, E], BF16, name="bias_rows")
+        bias_line = keep.tile([P, 2 * E], BF16, name="bias_line")
+        ones = keep.tile([P, P], BF16, name="ones")
+        identity_bf16 = keep.tile([P, P], BF16, name="identity_bf16")
         kv_codes = keep.tile([P, 2, E], U32, name="kv_codes", align_bytes=64)
         kv_scales = keep.tile([P, 2, E], U8, name="kv_scales", align_bytes=64)
 
         make_identity(nc, identity[:])
+        make_identity(nc, identity_bf16[:])
 
         raw_tiles = {}
 
         def load_piece(block, c):
             w, first_head, n_heads = BLOCKS[block]
             cols = n_heads * HD
-            if n_heads == 4:
-                raw = narrow_pool.tile([P, PACK, cols], BF16, name="raw_narrow")
-            else:
-                raw = wide_pool.tile([P, PACK, cols], BF16, name="raw_wide")
+            raw = raw_pool.tile([P, PACK, cols], BF16, name="raw")
             rows = weights[w].rearrange("(c p j) n -> c p j n", p=P, j=PACK)
             nc.sync.dma_start(
                 out=raw[:], in_=rows[c][:, :, first_head * HD : first_head * HD + cols]
             )
             raw_tiles[(block, c)] = raw
 
+        nc.gpsimd.memset(bias_line[:].bitcast(U32), 0)
+        nc.gpsimd.memset(ones[:], 1.0)
+
         def load_bias(w):
-            nc.sync.dma_start(out=bias_rows[:, w, :], in_=biases[w].partition_broadcast(P))
+            nc.sync.dma_start(
+                out=bias_line[0:1, w * E : (w + 1) * E], in_=biases[w].unsqueeze(0)
+            )
 
-        x_rows = hidden_states[0].rearrange("(p t) h -> p t h", t=ROW_TILES)
+        def spread_bias(w):
+            for half in range(2):
+                bank = move_banks.tile([P, 2 * BANK], BF16, name="move_bank")
+                for i in range(2):
+                    cols = slice(i * BANK, (i + 1) * BANK)
+                    line = slice(w * E + half * 2 * BANK + i * BANK, w * E + half * 2 * BANK + (i + 1) * BANK)
+                    nc.tensor.matmul(
+                        bank[:, cols], lhsT=ones[:], rhs=bias_line[:, line], start=True, stop=True
+                    )
+                nc.scalar.copy(
+                    out=bias_rows[:, w, half * 2 * BANK : (half + 1) * 2 * BANK], in_=bank[:]
+                )
 
-        def load_x(t):
-            nc.sync.dma_start(out=x_raw[:, t, :], in_=x_rows[:, t, :])
+        x_rows = hidden_states[0].rearrange("(p t) (c h) -> c p t h", t=ROW_TILES, c=PASSES)
+
+        x_tiles = []
+
+        def load_x(c):
+            x_raw = raw_pool.tile([P, ROW_TILES, K_PASS], BF16, name="raw")
+            nc.sync.dma_start(out=x_raw[:], in_=x_rows[c])
+            x_tiles.append(x_raw)
 
         load_piece(0, 0)
+        load_x(0)
         load_piece(0, 1)
-        for t in range(ROW_TILES):
-            load_x(t)
+        load_bias(0)
+        load_bias(1)
+        load_x(1)
+        load_x(2)
         load_piece(0, 2)
+        load_x(3)
         load_piece(0, 3)
         for c in range(PASSES):
             load_piece(1, c)
-        load_bias(0)
-        for c in range(PASSES):
-            load_piece(2, c)
-        load_bias(1)
-        for c in range(PASSES):
-            load_piece(3, c)
 
-        x_words = x_raw[:].bitcast(F32).rearrange(
-            "p t (c w u) -> p t c u w", c=PASSES, u=2
-        )
-        xg_words = x_grouped[:].bitcast(F32).rearrange(
-            "p (c t m u) -> p c t m u", c=PASSES, t=ROW_TILES, u=2
-        )
+        x_grouped = {}
 
-        def transpose_x(t):
+        def transpose_x(c):
+            x_words = x_tiles[c][:].bitcast(F32).rearrange("p t (w u) -> p t u w", u=2)
+            x_grouped[c] = heads_pool.tile(
+                [P, S * PACK], BF16, name="heads_grouped", align_bytes=64
+            )
+            xg_words = x_grouped[c][:].bitcast(F32).rearrange(
+                "p (t m u) -> p t m u", t=ROW_TILES, u=2
+            )
             for half in range(2):
                 bank = banks.tile([P, BANK], F32, name="bank")
-                planes = bank[:].rearrange("p (c u m) -> p c u m", c=2, u=2)
-                for c in range(2):
+                planes = bank[:].rearrange("p (t u m) -> p t u m", t=2, u=2)
+                for t in range(2):
                     for u in range(2):
                         nc.tensor.transpose(
-                            planes[:, c, u, :], x_words[:, t, 2 * half + c, u, :], identity[:]
+                            planes[:, t, u, :], x_words[:, 2 * half + t, u, :], identity[:]
                         )
                 copy = nc.scalar.copy if half == 0 else nc.vector.tensor_copy
                 copy(
-                    out=xg_words[:, 2 * half : 2 * half + 2, t, :, :],
-                    in_=planes.rearrange("p c u m -> p c m u"),
+                    out=xg_words[:, 2 * half : 2 * half + 2, :, :],
+                    in_=planes.rearrange("p t u m -> p t m u"),
                 )
 
         def quantise_x(c):
             nc.vector.quantize_mx(
                 out=x_codes[:, c, :].bitcast(FP8X4),
                 scales=x_scales[:, c, :],
-                in_=x_grouped[:, c * S * PACK : (c + 1) * S * PACK],
+                in_=x_grouped[c][:],
             )
 
         rounds = []
         last_round = {}
         for u, (block, first_head, n_heads) in enumerate(UNITS):
-            per_round = ROUND_COLS // (n_heads * HD)
+            per_round = min(ROUND_COLS // (n_heads * HD), PASSES)
             for c in range(0, PASSES, per_round):
                 last_round[u] = len(rounds)
                 rounds.append((u, range(c, c + per_round)))
+        moved = []
         grouped_tiles = {}
         wq_tiles = {}
         bank_tiles = {}
         head_tiles = {}
         state_tiles = {}
 
-        def regroup(r, scalar_cols):
+        def open_round(r):
+            u, passes = rounds[r]
+            cols = len(passes) * UNITS[u][2] * HD
+            grouped_tiles[r] = grouped_pool.tile(
+                [P, cols, PACK], BF16, name="grouped", align_bytes=64
+            )
+
+        def regroup_part(engine, r, i, lo, hi):
             u, passes = rounds[r]
             block, first_head, n_heads = UNITS[u]
             cols = n_heads * HD
             start = (first_head - BLOCKS[block][1]) * HD
-            grouped = grouped_pool.tile([P, ROUND_COLS, PACK], BF16, name="grouped", align_bytes=64)
-            for i, c in enumerate(passes):
-                raw = raw_tiles[(block, c)]
-                split = min(max(scalar_cols - i * cols, 0), cols)
-                for copy, lo, hi in (
-                    (nc.scalar.copy, 0, split), (nc.vector.tensor_copy, split, cols),
-                ):
+            out_part = grouped_tiles[r][:, i * cols + lo : i * cols + hi, :]
+            in_part = raw_tiles[(block, passes[i])][:, :, start + lo : start + hi]
+            if engine == 3:
+                bank = move_banks.tile([P, 2 * BANK], BF16, name="move_bank")
+                n = (hi - lo) * PACK
+                for a in range(0, n, BANK):
+                    cols_a = slice(a // PACK, min(a + BANK, n) // PACK)
+                    nc.tensor.matmul(
+                        bank[:, a : min(a + BANK, n)],
+                        lhsT=identity_bf16[:],
+                        rhs=in_part[:, :, cols_a].rearrange("p j n -> p n j"),
+                        start=True,
+                        stop=True,
+                    )
+                moved.append((out_part.rearrange("p n j -> p (n j)"), bank[:, 0:n]))
+            elif engine == 2:
+                nc.gpsimd.tensor_scalar(
+                    out=out_part,
+                    in0=in_part.rearrange("p j n -> p n j"),
+                    scalar1=1.0,
+                    scalar2=0.0,
+                    op0=mybir.AluOpType.mult,
+                    op1=mybir.AluOpType.add,
+                )
+            else:
+                copy = nc.scalar.copy if engine == 0 else nc.vector.tensor_copy
+                copy(
+                    out=out_part.rearrange("p (g i) j -> p g j i", i=4),
+                    in_=in_part.rearrange("p j (g i) -> p g j i", i=4),
+                )
+
+        def regroup(engine, r, only=None):
+            u, passes = rounds[r]
+            cols = UNITS[u][2] * HD
+            if r < FIRST_ROUNDS:
+                shares = [share * cols // 1024 for share in SHARES_EARLY]
+                lo = sum(shares[:engine])
+                for i in range(len(passes)):
+                    if shares[engine] and only in (None, i):
+                        regroup_part(engine, r, i, lo, lo + shares[engine])
+            else:
+                last = UNITS[u][2] == 1
+                total = len(passes) * cols
+                shares = [share * total // 1024 for share in (SHARES_LAST if last else SHARES)]
+                first = sum(shares[:engine])
+                for i in range(len(passes)):
+                    lo = max(first - i * cols, 0)
+                    hi = min(first + shares[engine] - i * cols, cols)
                     if lo < hi:
-                        copy(
-                            out=grouped[:, i * cols + lo : i * cols + hi, :].rearrange(
-                                "p (g i) j -> p g j i", i=4
-                            ),
-                            in_=raw[:, :, start + lo : start + hi].rearrange(
-                                "p j (g i) -> p g j i", i=4
-                            ),
-                        )
-            grouped_tiles[r] = grouped
+                        regroup_part(engine, r, i, lo, hi)
 
         def quantise_weights(r):
             u, passes = rounds[r]
@@ -179,7 +242,7 @@ def tile_linearattention_pa_kernel(tc, hidden_states, Wk, bk, Wv, bv, out):
                 w_scales = wq_pool.tile([P, PASSES * cols], U8, name="w_scales", align_bytes=64)
                 wq_tiles[u] = (w_codes, w_scales)
             w_codes, w_scales = wq_tiles[u]
-            words = slice(passes[0] * cols, passes[0] * cols + ROUND_COLS)
+            words = slice(passes[0] * cols, (passes[0] + len(passes)) * cols)
             nc.vector.quantize_mx(
                 out=w_codes[:, words].bitcast(FP8X4),
                 scales=w_scales[:, words],
@@ -211,9 +274,9 @@ def tile_linearattention_pa_kernel(tc, hidden_states, Wk, bk, Wv, bv, out):
             head = first_head + local_head
             if local_head == 0:
                 head_tiles[u] = heads_pool.tile(
-                    [P, n_heads * HD, PACK], BF16, name="heads_grouped", align_bytes=64
+                    [P, n_heads * HD * PACK], BF16, name="heads_grouped", align_bytes=64
                 )
-            heads_grouped = head_tiles[u]
+            heads_grouped = head_tiles[u][:].rearrange("p (n t) -> p n t", t=ROW_TILES)
             place = local_head * HD
             nc.vector.tensor_tensor(
                 out=heads_grouped[:, place : place + HD, :],
@@ -231,7 +294,7 @@ def tile_linearattention_pa_kernel(tc, hidden_states, Wk, bk, Wv, bv, out):
             nc.vector.quantize_mx(
                 out=kv_codes[:, w, cols].bitcast(FP8X4),
                 scales=kv_scales[:, w, cols],
-                in_=head_tiles[u][:].rearrange("p n t -> p (n t)"),
+                in_=head_tiles[u][:],
             )
 
         def state(u):
@@ -262,38 +325,88 @@ def tile_linearattention_pa_kernel(tc, hidden_states, Wk, bk, Wv, bv, out):
         to_project = {}
         to_bias = {}
         to_finish = {}
+        to_state = {}
         to_store = {}
         for u, (block, first_head, n_heads) in enumerate(UNITS):
+            q = last_round[u] + 1
             for local_head in range(n_heads):
-                q = last_round[u] + 1 + local_head
+                q = last_round[u] + 1 + local_head // 2
                 to_project.setdefault(q, []).append((u, local_head))
                 to_bias.setdefault(q + 1, []).append((u, local_head))
             to_finish.setdefault(q + 2, []).append(u)
             if BLOCKS[block][0] == 1:
-                to_store.setdefault(q + 2 + STORE_LAG, []).append(u)
-        n_rounds = max(to_store) + 1
-        late_blocks = [(block, c) for block in (4, 5) for c in range(PASSES)]
-        for q in range(n_rounds):
-            if 0 < q <= len(rounds):
-                quantise_weights(q - 1)
+                to_state.setdefault(q + 3, []).append(u)
+                to_store.setdefault(q + 3 + STORE_LAG, []).append(u)
+
+        def first_stage(q):
+            open_round(q)
+            regroup(2, q)
+
+        def unload_moved():
+            while moved:
+                target, source = moved.pop(0)
+                nc.scalar.copy(out=target, in_=source)
+
+        def second_stage(q):
+            regroup(3, q)
+            regroup(0, q)
+            unload_moved()
+
+        open_round(0)
+        open_round(1)
+        for i in range(2):
+            for engine in (3, 2, 0, 1):
+                regroup(engine, 0, i)
+            unload_moved()
+            transpose_x(i)
+        quantise_weights(0)
+        quantise_x(0)
+        quantise_x(1)
+        transpose_x(2)
+        for engine in (3, 2, 0, 1):
+            regroup(engine, 1, 0)
+        unload_moved()
+        quantise_x(2)
+        transpose_x(3)
+        for engine in (3, 2, 0, 1):
+            regroup(engine, 1, 1)
+        unload_moved()
+        spread_bias(0)
+        spread_bias(1)
+        quantise_x(3)
+        quantise_weights(1)
+        loads = [(block, c) for block in range(2, len(BLOCKS)) for c in range(PASSES)]
+
+        def load_more(n):
+            for i in range(n):
+                if loads:
+                    load_piece(*loads.pop(0))
+
+        load_more(20)
+        first_stage(2)
+        second_stage(2)
+        regroup(1, 2)
+        first_stage(3)
+        for q in range(2, max(to_store) + 1):
             for u in to_finish.get(q, []):
                 quantise_heads(u)
-            if q < len(rounds):
-                regroup(q, SCALAR_COLS_EARLY if q < 5 else SCALAR_COLS)
-            if q == 1:
-                for t in range(ROW_TILES):
-                    transpose_x(t)
-            if q == 2:
-                for c in range(PASSES):
-                    quantise_x(c)
-            if q >= 8 and late_blocks:
-                load_piece(*late_blocks.pop(0))
-            for u, local_head in to_project.get(q, []):
+            if 2 < q <= len(rounds):
+                quantise_weights(q - 1)
+            if q + AHEAD - 1 < len(rounds):
+                first_stage(q + AHEAD - 1)
+            load_more(2)
+            heads_now = to_project.get(q, [])
+            for u, local_head in heads_now[:1]:
                 project(u, local_head)
-            for u in to_finish.get(q, []):
-                if BLOCKS[UNITS[u][0]][0] == 1:
-                    state(u)
+            if q + 1 < len(rounds):
+                second_stage(q + 1)
+            for u, local_head in heads_now[1:]:
+                project(u, local_head)
+            for u in to_state.get(q, []):
+                state(u)
             for u, local_head in to_bias.get(q, []):
                 add_bias(u, local_head)
+            if q + 1 < len(rounds):
+                regroup(1, q + 1)
             for u in to_store.get(q, []):
                 store_state(u)

@@ -33,7 +33,7 @@ UNITS = (
 ROUND_COLS = 1024
 FIRST_ROUNDS = 3
 SHARES_EARLY = (512, 512, 0, 0)
-SHARES = (704, 320, 0, 0)
+SHARES = (640, 192, 192, 0)
 SHARES_LAST = (640, 384, 0, 0)
 AHEAD = 3
 STORE_LAG = 1

@@ -210,8 +210,8 @@ def tile_linearattention_pa_kernel(tc, hidden_states, Wk, bk, Wv, bv, out):
             else:
                 copy = nc.scalar.copy if engine == 0 else nc.vector.tensor_copy
                 copy(
-                    out=out_part.rearrange("p (g i) j -> p g j i", i=4),
-                    in_=in_part.rearrange("p j (g i) -> p g j i", i=4),
+                    out=out_part.rearrange("p (g i) j -> p g j i", i=8),
+                    in_=in_part.rearrange("p j (g i) -> p g j i", i=8),
                 )
 
         def regroup(engine, r, only=None):

from contextlib import ExitStack

import concourse.mybir as mybir
from concourse.masks import make_identity

BF16 = mybir.dt.bfloat16
F32 = mybir.dt.float32
U32 = mybir.dt.uint32
U8 = mybir.dt.uint8
FP8X4 = mybir.dt.float8_e4m3fn_x4

P = 128
PACK = 4
K_PASS = P * PACK

S = 512
H = 2048
HEADS = 16
HD = 128
E = HEADS * HD

PASSES = H // K_PASS
ROW_TILES = S // P
BANK = 512

BLOCKS = ((0, 0, 4), (1, 0, 4), (0, 4, 4), (1, 4, 4), (0, 8, 4), (1, 8, 4), (0, 12, 4), (1, 12, 4))

UNITS = (
    (0, 0, 4), (1, 0, 4), (2, 4, 4), (3, 4, 4), (4, 8, 4), (5, 8, 4), (6, 12, 4),
    (7, 12, 2), (7, 14, 1), (7, 15, 1),
)

ROUND_COLS = 1024
FIRST_ROUNDS = 3
SHARES_EARLY = (512, 512, 0, 0)
SHARES = (640, 192, 192, 0)
SHARES_LAST = (640, 384, 0, 0)
AHEAD = 3
STORE_LAG = 1

FLOPS = 2 * S * H * 2 * E + 2 * HEADS * HD * HD * S


def tile_linearattention_pa_kernel(tc, hidden_states, Wk, bk, Wv, bv, out):
    nc = tc.nc
    weights = (Wk, Wv)
    biases = (bk, bv)

    with ExitStack() as ctx:
        keep = ctx.enter_context(tc.tile_pool(name="keep", bufs=1))
        raw_pool = ctx.enter_context(tc.tile_pool(name="raw", bufs=24))
        grouped_pool = ctx.enter_context(tc.tile_pool(name="grouped", bufs=AHEAD))
        wq_pool = ctx.enter_context(tc.tile_pool(name="wq", bufs=2))
        heads_pool = ctx.enter_context(tc.tile_pool(name="heads", bufs=4))
        result_pool = ctx.enter_context(tc.tile_pool(name="result", bufs=4))
        banks = ctx.enter_context(tc.psum_pool(name="banks", bufs=5))
        move_banks = ctx.enter_context(tc.psum_pool(name="move_banks", bufs=2))
        state_banks = ctx.enter_context(tc.psum_pool(name="state_banks", bufs=1))
        ctx.enter_context(tc.manual_schedule())

        identity = keep.tile([P, P], F32, name="identity")
        x_codes = keep.tile([P, PASSES, S], U32, name="x_codes", align_bytes=64)
        x_scales = keep.tile([P, PASSES, S], U8, name="x_scales", align_bytes=64)
        bias_rows = keep.tile([P, 2, E], BF16, name="bias_rows")
        bias_line = keep.tile([P, 2 * E], BF16, name="bias_line")
        ones = keep.tile([P, P], BF16, name="ones")
        identity_bf16 = keep.tile([P, P], BF16, name="identity_bf16")
        kv_codes = keep.tile([P, 2, E], U32, name="kv_codes", align_bytes=64)
        kv_scales = keep.tile([P, 2, E], U8, name="kv_scales", align_bytes=64)

        make_identity(nc, identity[:])
        make_identity(nc, identity_bf16[:])

        raw_tiles = {}

        def load_piece(block, c):
            w, first_head, n_heads = BLOCKS[block]
            cols = n_heads * HD
            raw = raw_pool.tile([P, PACK, cols], BF16, name="raw")
            rows = weights[w].rearrange("(c p j) n -> c p j n", p=P, j=PACK)
            nc.sync.dma_start(
                out=raw[:], in_=rows[c][:, :, first_head * HD : first_head * HD + cols]
            )
            raw_tiles[(block, c)] = raw

        nc.gpsimd.memset(bias_line[:].bitcast(U32), 0)
        nc.gpsimd.memset(ones[:], 1.0)

        def load_bias(w):
            nc.sync.dma_start(
                out=bias_line[0:1, w * E : (w + 1) * E], in_=biases[w].unsqueeze(0)
            )

        def spread_bias(w):
            for half in range(2):
                bank = move_banks.tile([P, 2 * BANK], BF16, name="move_bank")
                for i in range(2):
                    cols = slice(i * BANK, (i + 1) * BANK)
                    line = slice(w * E + half * 2 * BANK + i * BANK, w * E + half * 2 * BANK + (i + 1) * BANK)
                    nc.tensor.matmul(
                        bank[:, cols], lhsT=ones[:], rhs=bias_line[:, line], start=True, stop=True
                    )
                nc.scalar.copy(
                    out=bias_rows[:, w, half * 2 * BANK : (half + 1) * 2 * BANK], in_=bank[:]
                )

        x_rows = hidden_states[0].rearrange("(p t) (c h) -> c p t h", t=ROW_TILES, c=PASSES)

        x_tiles = []

        def load_x(c):
            x_raw = raw_pool.tile([P, ROW_TILES, K_PASS], BF16, name="raw")
            nc.sync.dma_start(out=x_raw[:], in_=x_rows[c])
            x_tiles.append(x_raw)

        load_piece(0, 0)
        load_x(0)
        load_piece(0, 1)
        load_bias(0)
        load_bias(1)
        load_x(1)
        load_x(2)
        load_piece(0, 2)
        load_x(3)
        load_piece(0, 3)
        for c in range(PASSES):
            load_piece(1, c)

        x_grouped = {}

        def transpose_x(c):
            x_words = x_tiles[c][:].bitcast(F32).rearrange("p t (w u) -> p t u w", u=2)
            x_grouped[c] = heads_pool.tile(
                [P, S * PACK], BF16, name="heads_grouped", align_bytes=64
            )
            xg_words = x_grouped[c][:].bitcast(F32).rearrange(
                "p (t m u) -> p t m u", t=ROW_TILES, u=2
            )
            for half in range(2):
                bank = banks.tile([P, BANK], F32, name="bank")
                planes = bank[:].rearrange("p (t u m) -> p t u m", t=2, u=2)
                for t in range(2):
                    for u in range(2):
                        nc.tensor.transpose(
                            planes[:, t, u, :], x_words[:, 2 * half + t, u, :], identity[:]
                        )
                copy = nc.scalar.copy if half == 0 else nc.vector.tensor_copy
                copy(
                    out=xg_words[:, 2 * half : 2 * half + 2, :, :],
                    in_=planes.rearrange("p t u m -> p t m u"),
                )

        def quantise_x(c):
            nc.vector.quantize_mx(
                out=x_codes[:, c, :].bitcast(FP8X4),
                scales=x_scales[:, c, :],
                in_=x_grouped[c][:],
            )

        rounds = []
        last_round = {}
        for u, (block, first_head, n_heads) in enumerate(UNITS):
            per_round = min(ROUND_COLS // (n_heads * HD), PASSES)
            for c in range(0, PASSES, per_round):
                last_round[u] = len(rounds)
                rounds.append((u, range(c, c + per_round)))
        moved = []
        grouped_tiles = {}
        wq_tiles = {}
        bank_tiles = {}
        head_tiles = {}
        state_tiles = {}

        def open_round(r):
            u, passes = rounds[r]
            cols = len(passes) * UNITS[u][2] * HD
            grouped_tiles[r] = grouped_pool.tile(
                [P, cols, PACK], BF16, name="grouped", align_bytes=64
            )

        def regroup_part(engine, r, i, lo, hi):
            u, passes = rounds[r]
            block, first_head, n_heads = UNITS[u]
            cols = n_heads * HD
            start = (first_head - BLOCKS[block][1]) * HD
            out_part = grouped_tiles[r][:, i * cols + lo : i * cols + hi, :]
            in_part = raw_tiles[(block, passes[i])][:, :, start + lo : start + hi]
            if engine == 3:
                bank = move_banks.tile([P, 2 * BANK], BF16, name="move_bank")
                n = (hi - lo) * PACK
                for a in range(0, n, BANK):
                    cols_a = slice(a // PACK, min(a + BANK, n) // PACK)
                    nc.tensor.matmul(
                        bank[:, a : min(a + BANK, n)],
                        lhsT=identity_bf16[:],
                        rhs=in_part[:, :, cols_a].rearrange("p j n -> p n j"),
                        start=True,
                        stop=True,
                    )
                moved.append((out_part.rearrange("p n j -> p (n j)"), bank[:, 0:n]))
            elif engine == 2:
                nc.gpsimd.tensor_scalar(
                    out=out_part,
                    in0=in_part.rearrange("p j n -> p n j"),
                    scalar1=1.0,
                    scalar2=0.0,
                    op0=mybir.AluOpType.mult,
                    op1=mybir.AluOpType.add,
                )
            else:
                copy = nc.scalar.copy if engine == 0 else nc.vector.tensor_copy
                copy(
                    out=out_part.rearrange("p (g i) j -> p g j i", i=8),
                    in_=in_part.rearrange("p j (g i) -> p g j i", i=8),
                )

        def regroup(engine, r, only=None):
            u, passes = rounds[r]
            cols = UNITS[u][2] * HD
            if r < FIRST_ROUNDS:
                shares = [share * cols // 1024 for share in SHARES_EARLY]
                lo = sum(shares[:engine])
                for i in range(len(passes)):
                    if shares[engine] and only in (None, i):
                        regroup_part(engine, r, i, lo, lo + shares[engine])
            else:
                last = UNITS[u][2] == 1
                total = len(passes) * cols
                shares = [share * total // 1024 for share in (SHARES_LAST if last else SHARES)]
                first = sum(shares[:engine])
                for i in range(len(passes)):
                    lo = max(first - i * cols, 0)
                    hi = min(first + shares[engine] - i * cols, cols)
                    if lo < hi:
                        regroup_part(engine, r, i, lo, hi)

        def quantise_weights(r):
            u, passes = rounds[r]
            cols = UNITS[u][2] * HD
            if passes[0] == 0:
                w_codes = wq_pool.tile([P, PASSES * cols], U32, name="w_codes", align_bytes=64)
                w_scales = wq_pool.tile([P, PASSES * cols], U8, name="w_scales", align_bytes=64)
                wq_tiles[u] = (w_codes, w_scales)
            w_codes, w_scales = wq_tiles[u]
            words = slice(passes[0] * cols, (passes[0] + len(passes)) * cols)
            nc.vector.quantize_mx(
                out=w_codes[:, words].bitcast(FP8X4),
                scales=w_scales[:, words],
                in_=grouped_tiles[r][:].rearrange("p n j -> p (n j)"),
            )

        def project(u, local_head):
            w_codes, w_scales = wq_tiles[u]
            cols = UNITS[u][2] * HD
            bank = banks.tile([P, BANK], F32, name="bank")
            for t in range(ROW_TILES):
                rows = slice(t * P, (t + 1) * P)
                for c in range(PASSES):
                    words = slice(c * cols + local_head * HD, c * cols + (local_head + 1) * HD)
                    nc.tensor.matmul_mx(
                        out=bank[:, t * HD : (t + 1) * HD],
                        lhsT=x_codes[:, c, rows].bitcast(FP8X4),
                        lhsT_scale=x_scales[:, c, rows],
                        rhs=w_codes[:, words].bitcast(FP8X4),
                        rhs_scale=w_scales[:, words],
                        start=(c == 0),
                        stop=(c == PASSES - 1),
                    )
            bank_tiles[(u, local_head)] = bank

        def add_bias(u, local_head):
            block, first_head, n_heads = UNITS[u]
            w = BLOCKS[block][0]
            head = first_head + local_head
            if local_head == 0:
                head_tiles[u] = heads_pool.tile(
                    [P, n_heads * HD * PACK], BF16, name="heads_grouped", align_bytes=64
                )
            heads_grouped = head_tiles[u][:].rearrange("p (n t) -> p n t", t=ROW_TILES)
            place = local_head * HD
            nc.vector.tensor_tensor(
                out=heads_grouped[:, place : place + HD, :],
                in0=bank_tiles[(u, local_head)][:].rearrange("p (t n) -> p n t", t=ROW_TILES),
                in1=bias_rows[:, w, head * HD : (head + 1) * HD]
                .unsqueeze(2)
                .to_broadcast([P, HD, PACK]),
                op=mybir.AluOpType.add,
            )

        def quantise_heads(u):
            block, first_head, n_heads = UNITS[u]
            w = BLOCKS[block][0]
            cols = slice(first_head * HD, (first_head + n_heads) * HD)
            nc.vector.quantize_mx(
                out=kv_codes[:, w, cols].bitcast(FP8X4),
                scales=kv_scales[:, w, cols],
                in_=head_tiles[u][:],
            )

        def state(u):
            block, first_head, n_heads = UNITS[u]
            bank = state_banks.tile([P, n_heads, HD], F32, name="state_bank")
            for g in range(n_heads):
                cols = slice((first_head + g) * HD, (first_head + g + 1) * HD)
                nc.tensor.matmul_mx(
                    out=bank[:, g, :],
                    lhsT=kv_codes[:, 0, cols].bitcast(FP8X4),
                    lhsT_scale=kv_scales[:, 0, cols],
                    rhs=kv_codes[:, 1, cols].bitcast(FP8X4),
                    rhs_scale=kv_scales[:, 1, cols],
                    start=True,
                    stop=True,
                )
            state_tiles[u] = bank

        def store_state(u):
            block, first_head, n_heads = UNITS[u]
            result = result_pool.tile([P, n_heads, HD], F32, name="result")
            nc.scalar.copy(out=result[:], in_=state_tiles[u][:])
            nc.sync.dma_start(
                out=out[0, first_head : first_head + n_heads].rearrange("h d e -> d h e"),
                in_=result[:],
            )

        to_project = {}
        to_bias = {}
        to_finish = {}
        to_state = {}
        to_store = {}
        for u, (block, first_head, n_heads) in enumerate(UNITS):
            q = last_round[u] + 1
            for local_head in range(n_heads):
                q = last_round[u] + 1 + local_head // 2
                to_project.setdefault(q, []).append((u, local_head))
                to_bias.setdefault(q + 1, []).append((u, local_head))
            to_finish.setdefault(q + 2, []).append(u)
            if BLOCKS[block][0] == 1:
                to_state.setdefault(q + 3, []).append(u)
                to_store.setdefault(q + 3 + STORE_LAG, []).append(u)

        def first_stage(q):
            open_round(q)
            regroup(2, q)

        def unload_moved():
            while moved:
                target, source = moved.pop(0)
                nc.scalar.copy(out=target, in_=source)

        def second_stage(q):
            regroup(3, q)
            regroup(0, q)
            unload_moved()

        open_round(0)
        open_round(1)
        for i in range(2):
            for engine in (3, 2, 0, 1):
                regroup(engine, 0, i)
            unload_moved()
            transpose_x(i)
        quantise_weights(0)
        quantise_x(0)
        quantise_x(1)
        transpose_x(2)
        for engine in (3, 2, 0, 1):
            regroup(engine, 1, 0)
        unload_moved()
        quantise_x(2)
        transpose_x(3)
        for engine in (3, 2, 0, 1):
            regroup(engine, 1, 1)
        unload_moved()
        spread_bias(0)
        spread_bias(1)
        quantise_x(3)
        quantise_weights(1)
        loads = [(block, c) for block in range(2, len(BLOCKS)) for c in range(PASSES)]

        def load_more(n):
            for i in range(n):
                if loads:
                    load_piece(*loads.pop(0))

        load_more(20)
        first_stage(2)
        second_stage(2)
        regroup(1, 2)
        first_stage(3)
        for q in range(2, max(to_store) + 1):
            for u in to_finish.get(q, []):
                quantise_heads(u)
            if 2 < q <= len(rounds):
                quantise_weights(q - 1)
            if q + AHEAD - 1 < len(rounds):
                first_stage(q + AHEAD - 1)
            load_more(2)
            heads_now = to_project.get(q, [])
            for u, local_head in heads_now[:1]:
                project(u, local_head)
            if q + 1 < len(rounds):
                second_stage(q + 1)
            for u, local_head in heads_now[1:]:
                project(u, local_head)
            for u in to_state.get(q, []):
                state(u)
            for u, local_head in to_bias.get(q, []):
                add_bias(u, local_head)
            if q + 1 < len(rounds):
                regroup(1, q + 1)
            for u in to_store.get(q, []):
                store_state(u)
